import numpy as np
import ml_dtypes


def mxq(x, axis, fmt="e4m3"):
    dtype, down = {"e4m3": (ml_dtypes.float8_e4m3fn, 7), "e5m2": (ml_dtypes.float8_e5m2, 14)}[fmt]
    v = np.moveaxis(np.asarray(x, np.float32).astype(ml_dtypes.bfloat16).astype(np.float64), axis, -1)
    blocks = v.reshape(v.shape[:-1] + (-1, 32))
    amax = np.abs(blocks).max(-1, keepdims=True)
    byte = np.maximum(np.where(amax > 0, np.frexp(amax)[1] - 1 + 127, 0) - down, 1)
    scale = np.exp2(byte - 127.0)
    codes = (blocks / scale).astype(np.float32).astype(dtype).astype(np.float64)
    return np.moveaxis((codes * scale).reshape(v.shape), -1, axis)


WIDE = False


def mx_kscale(k):
    if not WIDE:
        return np.ones(k)
    levels = np.array([20, -20, 10, -10, 0])
    a = np.random.permutation(np.resize(levels, k // 512 * 4)).reshape(k // 512, 4)
    idx = np.arange(k)
    return np.exp2(a[idx // 512, idx % 128 // 32])


BF16 = ml_dtypes.bfloat16


def bf(x):
    return np.asarray(x, np.float32).astype(BF16)


def f64(x):
    return np.asarray(x).astype(np.float64)


B, A, C, P = 256, 3, 1024, 1024
N = A * A + 1


def scramble(y):
    return y.transpose(0, 2, 1).reshape(B, N, C)


def unscramble(z):
    return z.reshape(B, C, N).transpose(0, 2, 1)


def setup_inputs():
    u = mx_kscale(P)
    z = np.random.standard_normal((B, N, C)) * 1.6 / np.sqrt(N)
    w = np.random.standard_normal((P, C)) * 2.0 / np.sqrt(C) / u[:, None]
    b = np.random.standard_normal(P) * 0.1
    g = np.random.standard_normal((B, N, P)) * np.exp2(np.random.randint(-12, 1, (B, N, 1))) * 4.0 * u
    return {"y_attn": bf(np.ascontiguousarray(unscramble(z))),
            "w_proj": bf(w),
            "b_proj": bf(b),
            "grad_out": bf(g)}


def reference(y_attn, w_proj, b_proj, grad_out):
    gz = mxq(f64(grad_out), 2, "e5m2") @ mxq(f64(w_proj), 0, "e4m3")
    return np.ascontiguousarray(unscramble(gz))

@@ -1,0 +1,185 @@
+from contextlib import ExitStack
+
+import concourse.mybir as mybir
+from concourse.masks import make_identity
+
+F32 = mybir.dt.float32
+BF16 = mybir.dt.bfloat16
+U32 = mybir.dt.uint32
+U8 = mybir.dt.uint8
+E4M3X4 = mybir.dt.float8_e4m3fn_x4
+E5M2X4 = mybir.dt.float8_e5m2_x4
+
+PARTS = 128
+BATCH = 256
+TOKENS = 10
+CHANNELS = 1024
+FEATURES = 1024
+K_PASS = 512
+PASSES = FEATURES // K_PASS
+BANK = 512
+HALVES = BATCH // PARTS
+FIVE = TOKENS // 2
+UNIT_TOKENS = 5
+UNITS = HALVES * TOKENS // UNIT_TOKENS
+TILES = HALVES * TOKENS
+ROUND = 2
+VECTOR_COLS = 320
+
+FLOPS = 2 * BATCH * TOKENS * FEATURES * CHANNELS
+BYTES = 2 * BATCH * TOKENS * FEATURES + 2 * FEATURES * CHANNELS + 4 * BATCH * TOKENS * CHANNELS
+
+
+def tile_attention_pa_kernel(tc, y_attn, w_proj, b_proj, grad_out, out):
+    nc = tc.nc
+    with ExitStack() as ctx:
+        keep = ctx.enter_context(tc.tile_pool(name="keep", bufs=1))
+        stage = ctx.enter_context(tc.tile_pool(name="stage", bufs=4))
+        operands = ctx.enter_context(tc.tile_pool(name="operands", bufs=3 * ROUND))
+        results = ctx.enter_context(tc.tile_pool(name="results", bufs=4))
+        psum_t = ctx.enter_context(tc.psum_pool(name="psum_t", bufs=4))
+        psum_acc = ctx.enter_context(tc.psum_pool(name="psum_acc", bufs=4))
+        ctx.enter_context(tc.manual_schedule())
+
+        w_raw = keep.tile([PARTS, PASSES, 4, CHANNELS], BF16)
+        g_raw = [keep.tile([PARTS, TOKENS * FEATURES], BF16, name="g_raw%d" % h) for h in range(HALVES)]
+
+        def load_w(g):
+            for u in range(2):
+                rows = w_proj[K_PASS * g + 256 * u : K_PASS * g + 256 * u + 256, :]
+                nc.sync.dma_start(
+                    out=w_raw[:, g, 2 * u : 2 * u + 2, :],
+                    in_=rows.rearrange("(q e) j -> q e j", e=2),
+                )
+
+        def load_g(first_tile):
+            h, i = divmod(first_tile, TOKENS)
+            nc.sync.dma_start(
+                out=g_raw[h][:, FEATURES * i : FEATURES * (i + ROUND)],
+                in_=grad_out[PARTS * h : PARTS * (h + 1), i : i + ROUND, :].rearrange("b i p -> b (i p)"),
+            )
+
+        load_w(0)
+        load_g(0)
+        load_w(1)
+        for first_tile in range(ROUND, TILES, ROUND):
+            load_g(first_tile)
+
+        identity = keep.tile([PARTS, PARTS], F32)
+        make_identity(nc, identity[:])
+
+        w_grouped = keep.tile([PARTS, 2, PASSES, BANK, 4], BF16, align_bytes=64)
+        w_codes = keep.tile([PARTS, 2, PASSES, BANK], U32, align_bytes=64)
+        w_scales = keep.tile([PARTS, 2, PASSES, BANK], U8, align_bytes=64)
+
+        def regroup_w(parity, g):
+            source = w_raw[:, g, :, :].rearrange("q t (c two) -> q two c t", two=2)[:, parity]
+            target = w_grouped[:, parity, g, :, :]
+            nc.vector.tensor_copy(out=target[:, :VECTOR_COLS, :], in_=source[:, :VECTOR_COLS, :])
+            nc.scalar.copy(out=target[:, VECTOR_COLS:, :], in_=source[:, VECTOR_COLS:, :])
+
+        def quantise_w(parity, g):
+            nc.vector.quantize_mx(
+                out=w_codes[:, parity, g, :].bitcast(E4M3X4),
+                scales=w_scales[:, parity, g, :],
+                in_=w_grouped[:, parity, g, :, :].rearrange("q c t -> q (c t)"),
+            )
+
+        def transpose_tile(tile_index):
+            h, i = divmod(tile_index, TOKENS)
+            words = g_raw[h][:].bitcast(F32)
+            flipped = psum_t.tile([PARTS, 2 * PASSES, PARTS], F32)
+            for plane in range(2 * PASSES):
+                first_word = (FEATURES // 2) * i + PARTS * plane
+                nc.tensor.transpose(flipped[:, plane, :], words[:, first_word : first_word + PARTS], identity[:])
+            g_grouped = stage.tile([PARTS, PASSES * PARTS * 4], BF16, align_bytes=64)
+            nc.scalar.copy(
+                out=g_grouped[:].bitcast(F32).rearrange("q (g b u) -> q g b u", g=PASSES, u=2),
+                in_=flipped[:].rearrange("q (g u) b -> q g b u", u=2),
+            )
+            g_codes = operands.tile([PARTS, PASSES, PARTS], U32, align_bytes=64)
+            g_scales = operands.tile([PARTS, PASSES, PARTS], U8, align_bytes=64)
+            nc.vector.quantize_mx(
+                out=g_codes[:].rearrange("q g b -> q (g b)").bitcast(E5M2X4),
+                scales=g_scales[:].rearrange("q g b -> q (g b)"),
+                in_=g_grouped[:],
+            )
+            return g_codes, g_scales
+
+        def unscramble(parity, acc, unit_out, row):
+            copy = nc.vector.tensor_copy if parity == 0 else nc.scalar.copy
+            tokens = unit_out[:].rearrange("b (n two) c -> b two n c", two=2)[:, parity]
+            first = BANK * row
+            head = (-first) % FIVE
+            groups = (BANK - head) // FIVE
+            tail = BANK - head - FIVE * groups
+            channel = (first + head) // FIVE
+            if head:
+                copy(out=tokens[:, FIVE - head :, channel - 1], in_=acc[:, :head])
+            copy(
+                out=tokens[:, :, channel : channel + groups],
+                in_=acc[:, head : head + FIVE * groups].rearrange("b (c n) -> b n c", n=FIVE),
+            )
+            if tail:
+                copy(out=tokens[:, :tail, channel + groups], in_=acc[:, BANK - tail :])
+
+        unit_outs = {}
+        stored_channels = {}
+
+        def store_finished(unit, rows_done):
+            finished = (BANK * rows_done // FIVE) // 8 * 8
+            first = stored_channels.get(unit, 0)
+            h, side = divmod(unit, 2)
+            nc.sync.dma_start(
+                out=out[PARTS * h : PARTS * (h + 1), :, BANK * side + first : BANK * side + finished],
+                in_=unit_outs[unit][:, :, first:finished],
+            )
+            stored_channels[unit] = finished
+
+        def multiply_round(tile_indices, quantised):
+            accs = {}
+            for g in range(PASSES):
+                for tile_index in tile_indices:
+                    g_codes, g_scales = quantised[tile_index]
+                    for parity in range(2):
+                        if g == 0:
+                            accs[tile_index, parity] = psum_acc.tile([PARTS, BANK], F32, name="acc")
+                        nc.tensor.matmul_mx(
+                            out=accs[tile_index, parity][:],
+                            lhsT=g_codes[:, g, :].bitcast(E5M2X4),
+                            lhsT_scale=g_scales[:, g, :],
+                            rhs=w_codes[:, parity, g, :].bitcast(E4M3X4),
+                            rhs_scale=w_scales[:, parity, g, :],
+                            start=(g == 0),
+                            stop=(g == PASSES - 1),
+                        )
+            for tile_index in tile_indices:
+                unit, row = divmod(tile_index, UNIT_TOKENS)
+                if unit not in unit_outs:
+                    unit_outs[unit] = results.tile([PARTS, TOKENS, BANK], F32, name="unit_out")
+                for parity in range(2):
+                    unscramble(parity, accs[tile_index, parity], unit_outs[unit], row)
+            last_unit, last_row = divmod(tile_indices[-1], UNIT_TOKENS)
+            for unit in sorted(set(tile_index // UNIT_TOKENS for tile_index in tile_indices)):
+                rows_done = last_row + 1 if unit == last_unit else UNIT_TOKENS
+                if rows_done == UNIT_TOKENS or unit == UNITS - 1:
+                    store_finished(unit, rows_done)
+
+        rounds = [list(range(first, first + ROUND)) for first in range(0, TILES, ROUND)]
+        quantised = {}
+
+        def transpose_round(tile_indices):
+            for tile_index in tile_indices:
+                quantised[tile_index] = transpose_tile(tile_index)
+
+        for g in range(PASSES):
+            for parity in range(2):
+                regroup_w(parity, g)
+            for parity in range(2):
+                quantise_w(parity, g)
+            if g == 0:
+                transpose_round(rounds[0])
+        for r in range(len(rounds)):
+            if r + 1 < len(rounds):
+                transpose_round(rounds[r + 1])
+            multiply_round(rounds[r], quantised)

@@ -18,13 +18,17 @@ FEATURES = 1024
 K_PASS = 512
 PASSES = FEATURES // K_PASS
 BANK = 512
+BANKS = 8
+SIDES = CHANNELS // BANK
 HALVES = BATCH // PARTS
-FIVE = TOKENS // 2
 UNIT_TOKENS = 5
 UNITS = HALVES * TOKENS // UNIT_TOKENS
 TILES = HALVES * TOKENS
-ROUND = 2
-VECTOR_COLS = 320
+RUN = 4
+LEAD = 2
+LOAD_TOKENS = 2
+VECTOR_COLS = 256
+STORE_ROWS = {0: (3, 5), 1: (3, 5), 2: (3, 5), 3: (2, 4, 5)}
 
 FLOPS = 2 * BATCH * TOKENS * FEATURES * CHANNELS
 BYTES = 2 * BATCH * TOKENS * FEATURES + 2 * FEATURES * CHANNELS + 4 * BATCH * TOKENS * CHANNELS
@@ -34,152 +38,214 @@ def tile_attention_pa_kernel(tc, y_attn, w_proj, b_proj, grad_out, out):
     nc = tc.nc
     with ExitStack() as ctx:
         keep = ctx.enter_context(tc.tile_pool(name="keep", bufs=1))
-        stage = ctx.enter_context(tc.tile_pool(name="stage", bufs=4))
-        operands = ctx.enter_context(tc.tile_pool(name="operands", bufs=3 * ROUND))
-        results = ctx.enter_context(tc.tile_pool(name="results", bufs=4))
-        psum_t = ctx.enter_context(tc.psum_pool(name="psum_t", bufs=4))
-        psum_acc = ctx.enter_context(tc.psum_pool(name="psum_acc", bufs=4))
+        stage = ctx.enter_context(tc.tile_pool(name="stage", bufs=6))
+        psum = ctx.enter_context(tc.psum_pool(name="psum", bufs=1))
         ctx.enter_context(tc.manual_schedule())
 
         w_raw = keep.tile([PARTS, PASSES, 4, CHANNELS], BF16)
         g_raw = [keep.tile([PARTS, TOKENS * FEATURES], BF16, name="g_raw%d" % h) for h in range(HALVES)]
 
-        def load_w(g):
+        def load_w(side, g):
             for u in range(2):
-                rows = w_proj[K_PASS * g + 256 * u : K_PASS * g + 256 * u + 256, :]
+                rows = w_proj[K_PASS * g + 256 * u : K_PASS * g + 256 * u + 256, BANK * side : BANK * (side + 1)]
                 nc.sync.dma_start(
-                    out=w_raw[:, g, 2 * u : 2 * u + 2, :],
+                    out=w_raw[:, g, 2 * u : 2 * u + 2, BANK * side : BANK * (side + 1)],
                     in_=rows.rearrange("(q e) j -> q e j", e=2),
                 )
 
         def load_g(first_tile):
             h, i = divmod(first_tile, TOKENS)
             nc.sync.dma_start(
-                out=g_raw[h][:, FEATURES * i : FEATURES * (i + ROUND)],
-                in_=grad_out[PARTS * h : PARTS * (h + 1), i : i + ROUND, :].rearrange("b i p -> b (i p)"),
+                out=g_raw[h][:, FEATURES * i : FEATURES * (i + LOAD_TOKENS)],
+                in_=grad_out[PARTS * h : PARTS * (h + 1), i : i + LOAD_TOKENS, :].rearrange("b i p -> b (i p)"),
             )
 
-        load_w(0)
+        load_w(0, 0)
         load_g(0)
-        load_w(1)
-        for first_tile in range(ROUND, TILES, ROUND):
+        load_g(2)
+        load_w(0, 1)
+        load_w(1, 0)
+        load_w(1, 1)
+        for first_tile in range(RUN, TILES, LOAD_TOKENS):
             load_g(first_tile)
 
         identity = keep.tile([PARTS, PARTS], F32)
         make_identity(nc, identity[:])
 
-        w_grouped = keep.tile([PARTS, 2, PASSES, BANK, 4], BF16, align_bytes=64)
-        w_codes = keep.tile([PARTS, 2, PASSES, BANK], U32, align_bytes=64)
-        w_scales = keep.tile([PARTS, 2, PASSES, BANK], U8, align_bytes=64)
+        free_banks = list(range(BANKS))
 
-        def regroup_w(parity, g):
-            source = w_raw[:, g, :, :].rearrange("q t (c two) -> q two c t", two=2)[:, parity]
-            target = w_grouped[:, parity, g, :, :]
-            nc.vector.tensor_copy(out=target[:, :VECTOR_COLS, :], in_=source[:, :VECTOR_COLS, :])
-            nc.scalar.copy(out=target[:, VECTOR_COLS:, :], in_=source[:, VECTOR_COLS:, :])
+        def take_bank(shape):
+            bank = free_banks[0]
+            free_banks.remove(bank)
+            return bank, psum.tile(shape, F32, name="bank%d" % bank)
 
-        def quantise_w(parity, g):
+        w_grouped = keep.tile([PARTS, SIDES, PASSES, BANK, 4], BF16, align_bytes=64)
+        w_codes = keep.tile([PARTS, SIDES, PASSES, BANK], U32, align_bytes=64)
+        w_scales = keep.tile([PARTS, SIDES, PASSES, BANK], U8, align_bytes=64)
+
+        def regroup_w(side, g, copy, columns):
+            source = w_raw[:, g, :, BANK * side : BANK * (side + 1)].rearrange("q t c -> q c t")
+            copy(out=w_grouped[:, side, g, columns, :], in_=source[:, columns, :])
+
+        def regroup_v(side, g):
+            regroup_w(side, g, nc.vector.tensor_copy, slice(0, VECTOR_COLS))
+
+        def regroup_s(side, g):
+            regroup_w(side, g, nc.scalar.copy, slice(VECTOR_COLS, BANK))
+
+        def quantise_w(side, g):
             nc.vector.quantize_mx(
-                out=w_codes[:, parity, g, :].bitcast(E4M3X4),
-                scales=w_scales[:, parity, g, :],
-                in_=w_grouped[:, parity, g, :, :].rearrange("q c t -> q (c t)"),
+                out=w_codes[:, side, g, :].bitcast(E4M3X4),
+                scales=w_scales[:, side, g, :],
+                in_=w_grouped[:, side, g, :, :].rearrange("q c t -> q (c t)"),
             )
+
+        flipped = {}
+        grouped = {}
+        quantised = {}
 
         def transpose_tile(tile_index):
             h, i = divmod(tile_index, TOKENS)
             words = g_raw[h][:].bitcast(F32)
-            flipped = psum_t.tile([PARTS, 2 * PASSES, PARTS], F32)
+            bank, planes = take_bank([PARTS, 2 * PASSES, PARTS])
             for plane in range(2 * PASSES):
                 first_word = (FEATURES // 2) * i + PARTS * plane
-                nc.tensor.transpose(flipped[:, plane, :], words[:, first_word : first_word + PARTS], identity[:])
+                nc.tensor.transpose(planes[:, plane, :], words[:, first_word : first_word + PARTS], identity[:])
+            flipped[tile_index] = (bank, planes)
+
+        def empty_tile(tile_index, copy):
+            bank, planes = flipped[tile_index]
             g_grouped = stage.tile([PARTS, PASSES * PARTS * 4], BF16, align_bytes=64)
-            nc.scalar.copy(
+            copy(
                 out=g_grouped[:].bitcast(F32).rearrange("q (g b u) -> q g b u", g=PASSES, u=2),
-                in_=flipped[:].rearrange("q (g u) b -> q g b u", u=2),
+                in_=planes[:].rearrange("q (g u) b -> q g b u", u=2),
             )
-            g_codes = operands.tile([PARTS, PASSES, PARTS], U32, align_bytes=64)
-            g_scales = operands.tile([PARTS, PASSES, PARTS], U8, align_bytes=64)
+            free_banks.extend([bank])
+            grouped[tile_index] = g_grouped
+
+        def quantise_tile(tile_index):
+            g_grouped = grouped[tile_index]
+            g_codes = keep.tile([PARTS, PASSES, PARTS], U32, align_bytes=64, name="g_codes%d" % tile_index)
+            g_scales = keep.tile([PARTS, PASSES, PARTS], U8, align_bytes=64, name="g_scales%d" % tile_index)
             nc.vector.quantize_mx(
                 out=g_codes[:].rearrange("q g b -> q (g b)").bitcast(E5M2X4),
                 scales=g_scales[:].rearrange("q g b -> q (g b)"),
                 in_=g_grouped[:],
             )
-            return g_codes, g_scales
+            quantised[tile_index] = (g_codes, g_scales)
 
-        def unscramble(parity, acc, unit_out, row):
-            copy = nc.vector.tensor_copy if parity == 0 else nc.scalar.copy
-            tokens = unit_out[:].rearrange("b (n two) c -> b two n c", two=2)[:, parity]
-            first = BANK * row
-            head = (-first) % FIVE
-            groups = (BANK - head) // FIVE
-            tail = BANK - head - FIVE * groups
-            channel = (first + head) // FIVE
-            if head:
-                copy(out=tokens[:, FIVE - head :, channel - 1], in_=acc[:, :head])
-            copy(
-                out=tokens[:, :, channel : channel + groups],
-                in_=acc[:, head : head + FIVE * groups].rearrange("b (c n) -> b n c", n=FIVE),
+        accs = {}
+
+        def multiply(tile_index, side, g):
+            if g == 0:
+                accs[tile_index, side] = take_bank([PARTS, BANK])
+            g_codes, g_scales = quantised[tile_index]
+            nc.tensor.matmul_mx(
+                out=accs[tile_index, side][1][:],
+                lhsT=g_codes[:, g, :].bitcast(E5M2X4),
+                lhsT_scale=g_scales[:, g, :],
+                rhs=w_codes[:, side, g, :].bitcast(E4M3X4),
+                rhs_scale=w_scales[:, side, g, :],
+                start=(g == 0),
+                stop=(g == PASSES - 1),
             )
-            if tail:
-                copy(out=tokens[:, :tail, channel + groups], in_=acc[:, BANK - tail :])
 
         unit_outs = {}
         stored_channels = {}
 
-        def store_finished(unit, rows_done):
-            finished = (BANK * rows_done // FIVE) // 8 * 8
+        def unscramble(tile_index, side, copy):
+            bank, acc = accs[tile_index, side]
+            unit, row = divmod(tile_index, UNIT_TOKENS)
+            if unit not in unit_outs:
+                unit_outs[unit] = keep.tile([PARTS, TOKENS, BANK], F32, name="unit_out%d" % unit)
+            tokens = unit_outs[unit]
+            first = CHANNELS * row + BANK * side
+            head = (-first) % TOKENS
+            groups = (BANK - head) // TOKENS
+            tail = BANK - head - TOKENS * groups
+            channel = (first + head) // TOKENS
+            if head:
+                copy(out=tokens[:, TOKENS - head :, channel - 1], in_=acc[:, :head])
+            copy(
+                out=tokens[:, :, channel : channel + groups],
+                in_=acc[:, head : head + TOKENS * groups].rearrange("b (c n) -> b n c", n=TOKENS),
+            )
+            if tail:
+                copy(out=tokens[:, :tail, channel + groups], in_=acc[:, BANK - tail :])
+            free_banks.extend([bank])
+
+        def store_finished(tile_index):
+            unit, row = divmod(tile_index, UNIT_TOKENS)
+            rows_done = row + 1
+            if rows_done not in STORE_ROWS[unit]:
+                return
+            finished = (CHANNELS * rows_done // TOKENS) // 8 * 8
             first = stored_channels.get(unit, 0)
-            h, side = divmod(unit, 2)
+            h, s = divmod(unit, 2)
             nc.sync.dma_start(
-                out=out[PARTS * h : PARTS * (h + 1), :, BANK * side + first : BANK * side + finished],
+                out=out[PARTS * h : PARTS * (h + 1), :, BANK * s + first : BANK * s + finished],
                 in_=unit_outs[unit][:, :, first:finished],
             )
             stored_channels[unit] = finished
 
-        def multiply_round(tile_indices, quantised):
-            accs = {}
-            for g in range(PASSES):
-                for tile_index in tile_indices:
-                    g_codes, g_scales = quantised[tile_index]
-                    for parity in range(2):
-                        if g == 0:
-                            accs[tile_index, parity] = psum_acc.tile([PARTS, BANK], F32, name="acc")
-                        nc.tensor.matmul_mx(
-                            out=accs[tile_index, parity][:],
-                            lhsT=g_codes[:, g, :].bitcast(E5M2X4),
-                            lhsT_scale=g_scales[:, g, :],
-                            rhs=w_codes[:, parity, g, :].bitcast(E4M3X4),
-                            rhs_scale=w_scales[:, parity, g, :],
-                            start=(g == 0),
-                            stop=(g == PASSES - 1),
-                        )
-            for tile_index in tile_indices:
-                unit, row = divmod(tile_index, UNIT_TOKENS)
-                if unit not in unit_outs:
-                    unit_outs[unit] = results.tile([PARTS, TOKENS, BANK], F32, name="unit_out")
-                for parity in range(2):
-                    unscramble(parity, accs[tile_index, parity], unit_outs[unit], row)
-            last_unit, last_row = divmod(tile_indices[-1], UNIT_TOKENS)
-            for unit in sorted(set(tile_index // UNIT_TOKENS for tile_index in tile_indices)):
-                rows_done = last_row + 1 if unit == last_unit else UNIT_TOKENS
-                if rows_done == UNIT_TOKENS or unit == UNITS - 1:
-                    store_finished(unit, rows_done)
+        def finish_tile(tile_index):
+            unscramble(tile_index, 0, nc.vector.tensor_copy)
+            unscramble(tile_index, 1, nc.scalar.copy)
+            store_finished(tile_index)
 
-        rounds = [list(range(first, first + ROUND)) for first in range(0, TILES, ROUND)]
-        quantised = {}
+        def transpose_run(first_tile):
+            for tile_index in range(first_tile, first_tile + RUN):
+                transpose_tile(tile_index)
+            for tile_index in range(first_tile, first_tile + RUN):
+                empty_tile(tile_index, nc.vector.tensor_copy if tile_index == first_tile else nc.scalar.copy)
 
-        def transpose_round(tile_indices):
-            for tile_index in tile_indices:
-                quantised[tile_index] = transpose_tile(tile_index)
+        regroup_v(0, 0)
+        regroup_s(0, 0)
+        quantise_w(0, 0)
+        for tile_index in range(RUN):
+            transpose_tile(tile_index)
+        for tile_index in range(RUN):
+            empty_tile(tile_index, nc.scalar.copy)
+        quantise_tile(0)
+        quantise_tile(1)
+        regroup_v(0, 1)
+        quantise_tile(2)
+        quantise_tile(3)
+        for tile_index in range(RUN):
+            multiply(tile_index, 0, 0)
+        regroup_s(0, 1)
+        regroup_v(1, 0)
+        quantise_w(0, 1)
+        for tile_index in range(RUN):
+            multiply(tile_index, 0, 1)
+        regroup_s(1, 0)
+        regroup_v(1, 1)
+        quantise_w(1, 0)
+        for tile_index in range(RUN):
+            multiply(tile_index, 1, 0)
+        regroup_s(1, 1)
+        quantise_w(1, 1)
+        for tile_index in range(RUN):
+            multiply(tile_index, 1, 1)
+        for tile_index in range(RUN):
+            unscramble(tile_index, 0, nc.vector.tensor_copy if tile_index % 2 == 0 else nc.scalar.copy)
+        transpose_run(RUN)
+        for tile_index in range(RUN, 2 * RUN):
+            quantise_tile(tile_index)
+        for tile_index in range(RUN):
+            unscramble(tile_index, 1, nc.vector.tensor_copy if tile_index % 2 == 0 else nc.scalar.copy)
+            store_finished(tile_index)
 
-        for g in range(PASSES):
-            for parity in range(2):
-                regroup_w(parity, g)
-            for parity in range(2):
-                quantise_w(parity, g)
-            if g == 0:
-                transpose_round(rounds[0])
-        for r in range(len(rounds)):
-            if r + 1 < len(rounds):
-                transpose_round(rounds[r + 1])
-            multiply_round(rounds[r], quantised)
+        to_quantise = []
+        for tile_index in range(RUN, TILES):
+            ahead = tile_index + LEAD
+            if ahead % RUN == 0 and ahead >= 2 * RUN and ahead < TILES:
+                transpose_run(ahead)
+                to_quantise.extend(range(ahead, ahead + RUN))
+            for side in range(SIDES):
+                for g in range(PASSES):
+                    multiply(tile_index, side, g)
+            finish_tile(tile_index)
+            for waiting in to_quantise[: RUN // LEAD]:
+                quantise_tile(waiting)
+            to_quantise = to_quantise[RUN // LEAD :]

@@ -28,7 +28,7 @@ RUN = 4
 LEAD = 2
 LOAD_TOKENS = 2
 VECTOR_COLS = 256
-STORE_ROWS = {0: (3, 5), 1: (3, 5), 2: (3, 5), 3: (2, 4, 5)}
+STORE_ROWS = {0: (5,), 1: (5,), 2: (3, 5), 3: (3, 5)}
 
 FLOPS = 2 * BATCH * TOKENS * FEATURES * CHANNELS
 BYTES = 2 * BATCH * TOKENS * FEATURES + 2 * FEATURES * CHANNELS + 4 * BATCH * TOKENS * CHANNELS

@@ -28,7 +28,7 @@ RUN = 4
 LEAD = 2
 LOAD_TOKENS = 2
 VECTOR_COLS = 256
-STORE_ROWS = {0: (5,), 1: (5,), 2: (3, 5), 3: (3, 5)}
+PIECES = {0: (512,), 1: (512,), 2: (256, 512), 3: (256, 512)}
 
 FLOPS = 2 * BATCH * TOKENS * FEATURES * CHANNELS
 BYTES = 2 * BATCH * TOKENS * FEATURES + 2 * FEATURES * CHANNELS + 4 * BATCH * TOKENS * CHANNELS
@@ -176,17 +176,16 @@ def tile_attention_pa_kernel(tc, y_attn, w_proj, b_proj, grad_out, out):
 
         def store_finished(tile_index):
             unit, row = divmod(tile_index, UNIT_TOKENS)
-            rows_done = row + 1
-            if rows_done not in STORE_ROWS[unit]:
-                return
-            finished = (CHANNELS * rows_done // TOKENS) // 8 * 8
-            first = stored_channels.get(unit, 0)
+            complete = CHANNELS * (row + 1) // TOKENS
             h, s = divmod(unit, 2)
-            nc.sync.dma_start(
-                out=out[PARTS * h : PARTS * (h + 1), :, BANK * s + first : BANK * s + finished],
-                in_=unit_outs[unit][:, :, first:finished],
-            )
-            stored_channels[unit] = finished
+            for finished in PIECES[unit]:
+                first = stored_channels.get(unit, 0)
+                if first < finished and finished <= complete:
+                    nc.sync.dma_start(
+                        out=out[PARTS * h : PARTS * (h + 1), :, BANK * s + first : BANK * s + finished],
+                        in_=unit_outs[unit][:, :, first:finished],
+                    )
+                    stored_channels[unit] = finished
 
         def finish_tile(tile_index):
             unscramble(tile_index, 0, nc.vector.tensor_copy)

@@ -42,14 +42,17 @@ def tile_attention_pa_kernel(tc, y_attn, w_proj, b_proj, grad_out, out):
         psum = ctx.enter_context(tc.psum_pool(name="psum", bufs=1))
         ctx.enter_context(tc.manual_schedule())
 
-        w_raw = keep.tile([PARTS, PASSES, 4, CHANNELS], BF16)
+        w_raw = {}
+        for side in range(SIDES):
+            for g in range(PASSES):
+                w_raw[side, g] = keep.tile([PARTS, 4, BANK], BF16, name="w_raw%d%d" % (side, g))
         g_raw = [keep.tile([PARTS, TOKENS * FEATURES], BF16, name="g_raw%d" % h) for h in range(HALVES)]
 
         def load_w(side, g):
             for u in range(2):
                 rows = w_proj[K_PASS * g + 256 * u : K_PASS * g + 256 * u + 256, BANK * side : BANK * (side + 1)]
                 nc.sync.dma_start(
-                    out=w_raw[:, g, 2 * u : 2 * u + 2, BANK * side : BANK * (side + 1)],
+                    out=w_raw[side, g][:, 2 * u : 2 * u + 2, :],
                     in_=rows.rearrange("(q e) j -> q e j", e=2),
                 )
 
@@ -84,8 +87,10 @@ def tile_attention_pa_kernel(tc, y_attn, w_proj, b_proj, grad_out, out):
         w_scales = keep.tile([PARTS, SIDES, PASSES, BANK], U8, align_bytes=64)
 
         def regroup_w(side, g, copy, columns):
-            source = w_raw[:, g, :, BANK * side : BANK * (side + 1)].rearrange("q t c -> q c t")
-            copy(out=w_grouped[:, side, g, columns, :], in_=source[:, columns, :])
+            copy(
+                out=w_grouped[:, side, g, columns, :].rearrange("q (c i) t -> q c t i", i=4),
+                in_=w_raw[side, g][:, :, columns].rearrange("q t (c i) -> q c t i", i=4),
+            )
 
         def regroup_v(side, g):
             regroup_w(side, g, nc.vector.tensor_copy, slice(0, VECTOR_COLS))

@@ -88,8 +88,8 @@ def tile_attention_pa_kernel(tc, y_attn, w_proj, b_proj, grad_out, out):
 
         def regroup_w(side, g, copy, columns):
             copy(
-                out=w_grouped[:, side, g, columns, :].rearrange("q (c i) t -> q c t i", i=4),
-                in_=w_raw[side, g][:, :, columns].rearrange("q t (c i) -> q c t i", i=4),
+                out=w_grouped[:, side, g, columns, :].rearrange("q (c i) t -> q c t i", i=8),
+                in_=w_raw[side, g][:, :, columns].rearrange("q t (c i) -> q c t i", i=8),
             )
 
         def regroup_v(side, g):

@@ -25,6 +25,7 @@ UNIT_TOKENS = 5
 UNITS = HALVES * TOKENS // UNIT_TOKENS
 TILES = HALVES * TOKENS
 RUN = 4
+SHORT_RUN = 2
 LEAD = 2
 LOAD_TOKENS = 2
 VECTOR_COLS = 256
@@ -243,13 +244,16 @@ def tile_attention_pa_kernel(tc, y_attn, w_proj, b_proj, grad_out, out):
         to_quantise = []
         for tile_index in range(RUN, TILES):
             ahead = tile_index + LEAD
-            if ahead % RUN == 0 and ahead >= 2 * RUN and ahead < TILES:
-                transpose_run(ahead)
-                to_quantise.extend(range(ahead, ahead + RUN))
+            if ahead % SHORT_RUN == 0 and ahead >= 2 * RUN and ahead < TILES:
+                for coming in range(ahead, ahead + SHORT_RUN):
+                    transpose_tile(coming)
+                for coming in range(ahead, ahead + SHORT_RUN):
+                    empty_tile(coming, nc.vector.tensor_copy if coming % RUN == 0 else nc.scalar.copy)
+                to_quantise.extend(range(ahead, ahead + SHORT_RUN))
             for side in range(SIDES):
                 for g in range(PASSES):
                     multiply(tile_index, side, g)
             finish_tile(tile_index)
-            for waiting in to_quantise[: RUN // LEAD]:
+            for waiting in to_quantise[:1]:
                 quantise_tile(waiting)
-            to_quantise = to_quantise[RUN // LEAD :]
+            to_quantise = to_quantise[1:]

from contextlib import ExitStack

import concourse.mybir as mybir
from concourse.masks import make_identity

F32 = mybir.dt.float32
BF16 = mybir.dt.bfloat16
U32 = mybir.dt.uint32
U8 = mybir.dt.uint8
E4M3X4 = mybir.dt.float8_e4m3fn_x4
E5M2X4 = mybir.dt.float8_e5m2_x4

PARTS = 128
BATCH = 256
TOKENS = 10
CHANNELS = 1024
FEATURES = 1024
K_PASS = 512
PASSES = FEATURES // K_PASS
BANK = 512
BANKS = 8
SIDES = CHANNELS // BANK
HALVES = BATCH // PARTS
UNIT_TOKENS = 5
UNITS = HALVES * TOKENS // UNIT_TOKENS
TILES = HALVES * TOKENS
RUN = 4
SHORT_RUN = 2
LEAD = 2
LOAD_TOKENS = 2
VECTOR_COLS = 256
PIECES = {0: (512,), 1: (512,), 2: (256, 512), 3: (256, 512)}

FLOPS = 2 * BATCH * TOKENS * FEATURES * CHANNELS
BYTES = 2 * BATCH * TOKENS * FEATURES + 2 * FEATURES * CHANNELS + 4 * BATCH * TOKENS * CHANNELS


def tile_attention_pa_kernel(tc, y_attn, w_proj, b_proj, grad_out, out):
    nc = tc.nc
    with ExitStack() as ctx:
        keep = ctx.enter_context(tc.tile_pool(name="keep", bufs=1))
        stage = ctx.enter_context(tc.tile_pool(name="stage", bufs=6))
        psum = ctx.enter_context(tc.psum_pool(name="psum", bufs=1))
        ctx.enter_context(tc.manual_schedule())

        w_raw = {}
        for side in range(SIDES):
            for g in range(PASSES):
                w_raw[side, g] = keep.tile([PARTS, 4, BANK], BF16, name="w_raw%d%d" % (side, g))
        g_raw = [keep.tile([PARTS, TOKENS * FEATURES], BF16, name="g_raw%d" % h) for h in range(HALVES)]

        def load_w(side, g):
            for u in range(2):
                rows = w_proj[K_PASS * g + 256 * u : K_PASS * g + 256 * u + 256, BANK * side : BANK * (side + 1)]
                nc.sync.dma_start(
                    out=w_raw[side, g][:, 2 * u : 2 * u + 2, :],
                    in_=rows.rearrange("(q e) j -> q e j", e=2),
                )

        def load_g(first_tile):
            h, i = divmod(first_tile, TOKENS)
            nc.sync.dma_start(
                out=g_raw[h][:, FEATURES * i : FEATURES * (i + LOAD_TOKENS)],
                in_=grad_out[PARTS * h : PARTS * (h + 1), i : i + LOAD_TOKENS, :].rearrange("b i p -> b (i p)"),
            )

        load_w(0, 0)
        load_g(0)
        load_g(2)
        load_w(0, 1)
        load_w(1, 0)
        load_w(1, 1)
        for first_tile in range(RUN, TILES, LOAD_TOKENS):
            load_g(first_tile)

        identity = keep.tile([PARTS, PARTS], F32)
        make_identity(nc, identity[:])

        free_banks = list(range(BANKS))

        def take_bank(shape):
            bank = free_banks[0]
            free_banks.remove(bank)
            return bank, psum.tile(shape, F32, name="bank%d" % bank)

        w_grouped = keep.tile([PARTS, SIDES, PASSES, BANK, 4], BF16, align_bytes=64)
        w_codes = keep.tile([PARTS, SIDES, PASSES, BANK], U32, align_bytes=64)
        w_scales = keep.tile([PARTS, SIDES, PASSES, BANK], U8, align_bytes=64)

        def regroup_w(side, g, copy, columns):
            copy(
                out=w_grouped[:, side, g, columns, :].rearrange("q (c i) t -> q c t i", i=8),
                in_=w_raw[side, g][:, :, columns].rearrange("q t (c i) -> q c t i", i=8),
            )

        def regroup_v(side, g):
            regroup_w(side, g, nc.vector.tensor_copy, slice(0, VECTOR_COLS))

        def regroup_s(side, g):
            regroup_w(side, g, nc.scalar.copy, slice(VECTOR_COLS, BANK))

        def quantise_w(side, g):
            nc.vector.quantize_mx(
                out=w_codes[:, side, g, :].bitcast(E4M3X4),
                scales=w_scales[:, side, g, :],
                in_=w_grouped[:, side, g, :, :].rearrange("q c t -> q (c t)"),
            )

        flipped = {}
        grouped = {}
        quantised = {}

        def transpose_tile(tile_index):
            h, i = divmod(tile_index, TOKENS)
            words = g_raw[h][:].bitcast(F32)
            bank, planes = take_bank([PARTS, 2 * PASSES, PARTS])
            for plane in range(2 * PASSES):
                first_word = (FEATURES // 2) * i + PARTS * plane
                nc.tensor.transpose(planes[:, plane, :], words[:, first_word : first_word + PARTS], identity[:])
            flipped[tile_index] = (bank, planes)

        def empty_tile(tile_index, copy):
            bank, planes = flipped[tile_index]
            g_grouped = stage.tile([PARTS, PASSES * PARTS * 4], BF16, align_bytes=64)
            copy(
                out=g_grouped[:].bitcast(F32).rearrange("q (g b u) -> q g b u", g=PASSES, u=2),
                in_=planes[:].rearrange("q (g u) b -> q g b u", u=2),
            )
            free_banks.extend([bank])
            grouped[tile_index] = g_grouped

        def quantise_tile(tile_index):
            g_grouped = grouped[tile_index]
            g_codes = keep.tile([PARTS, PASSES, PARTS], U32, align_bytes=64, name="g_codes%d" % tile_index)
            g_scales = keep.tile([PARTS, PASSES, PARTS], U8, align_bytes=64, name="g_scales%d" % tile_index)
            nc.vector.quantize_mx(
                out=g_codes[:].rearrange("q g b -> q (g b)").bitcast(E5M2X4),
                scales=g_scales[:].rearrange("q g b -> q (g b)"),
                in_=g_grouped[:],
            )
            quantised[tile_index] = (g_codes, g_scales)

        accs = {}

        def multiply(tile_index, side, g):
            if g == 0:
                accs[tile_index, side] = take_bank([PARTS, BANK])
            g_codes, g_scales = quantised[tile_index]
            nc.tensor.matmul_mx(
                out=accs[tile_index, side][1][:],
                lhsT=g_codes[:, g, :].bitcast(E5M2X4),
                lhsT_scale=g_scales[:, g, :],
                rhs=w_codes[:, side, g, :].bitcast(E4M3X4),
                rhs_scale=w_scales[:, side, g, :],
                start=(g == 0),
                stop=(g == PASSES - 1),
            )

        unit_outs = {}
        stored_channels = {}

        def unscramble(tile_index, side, copy):
            bank, acc = accs[tile_index, side]
            unit, row = divmod(tile_index, UNIT_TOKENS)
            if unit not in unit_outs:
                unit_outs[unit] = keep.tile([PARTS, TOKENS, BANK], F32, name="unit_out%d" % unit)
            tokens = unit_outs[unit]
            first = CHANNELS * row + BANK * side
            head = (-first) % TOKENS
            groups = (BANK - head) // TOKENS
            tail = BANK - head - TOKENS * groups
            channel = (first + head) // TOKENS
            if head:
                copy(out=tokens[:, TOKENS - head :, channel - 1], in_=acc[:, :head])
            copy(
                out=tokens[:, :, channel : channel + groups],
                in_=acc[:, head : head + TOKENS * groups].rearrange("b (c n) -> b n c", n=TOKENS),
            )
            if tail:
                copy(out=tokens[:, :tail, channel + groups], in_=acc[:, BANK - tail :])
            free_banks.extend([bank])

        def store_finished(tile_index):
            unit, row = divmod(tile_index, UNIT_TOKENS)
            complete = CHANNELS * (row + 1) // TOKENS
            h, s = divmod(unit, 2)
            for finished in PIECES[unit]:
                first = stored_channels.get(unit, 0)
                if first < finished and finished <= complete:
                    nc.sync.dma_start(
                        out=out[PARTS * h : PARTS * (h + 1), :, BANK * s + first : BANK * s + finished],
                        in_=unit_outs[unit][:, :, first:finished],
                    )
                    stored_channels[unit] = finished

        def finish_tile(tile_index):
            unscramble(tile_index, 0, nc.vector.tensor_copy)
            unscramble(tile_index, 1, nc.scalar.copy)
            store_finished(tile_index)

        def transpose_run(first_tile):
            for tile_index in range(first_tile, first_tile + RUN):
                transpose_tile(tile_index)
            for tile_index in range(first_tile, first_tile + RUN):
                empty_tile(tile_index, nc.vector.tensor_copy if tile_index == first_tile else nc.scalar.copy)

        regroup_v(0, 0)
        regroup_s(0, 0)
        quantise_w(0, 0)
        for tile_index in range(RUN):
            transpose_tile(tile_index)
        for tile_index in range(RUN):
            empty_tile(tile_index, nc.scalar.copy)
        quantise_tile(0)
        quantise_tile(1)
        regroup_v(0, 1)
        quantise_tile(2)
        quantise_tile(3)
        for tile_index in range(RUN):
            multiply(tile_index, 0, 0)
        regroup_s(0, 1)
        regroup_v(1, 0)
        quantise_w(0, 1)
        for tile_index in range(RUN):
            multiply(tile_index, 0, 1)
        regroup_s(1, 0)
        regroup_v(1, 1)
        quantise_w(1, 0)
        for tile_index in range(RUN):
            multiply(tile_index, 1, 0)
        regroup_s(1, 1)
        quantise_w(1, 1)
        for tile_index in range(RUN):
            multiply(tile_index, 1, 1)
        for tile_index in range(RUN):
            unscramble(tile_index, 0, nc.vector.tensor_copy if tile_index % 2 == 0 else nc.scalar.copy)
        transpose_run(RUN)
        for tile_index in range(RUN, 2 * RUN):
            quantise_tile(tile_index)
        for tile_index in range(RUN):
            unscramble(tile_index, 1, nc.vector.tensor_copy if tile_index % 2 == 0 else nc.scalar.copy)
            store_finished(tile_index)

        to_quantise = []
        for tile_index in range(RUN, TILES):
            ahead = tile_index + LEAD
            if ahead % SHORT_RUN == 0 and ahead >= 2 * RUN and ahead < TILES:
                for coming in range(ahead, ahead + SHORT_RUN):
                    transpose_tile(coming)
                for coming in range(ahead, ahead + SHORT_RUN):
                    empty_tile(coming, nc.vector.tensor_copy if coming % RUN == 0 else nc.scalar.copy)
                to_quantise.extend(range(ahead, ahead + SHORT_RUN))
            for side in range(SIDES):
                for g in range(PASSES):
                    multiply(tile_index, side, g)
            finish_tile(tile_index)
            for waiting in to_quantise[:1]:
                quantise_tile(waiting)
            to_quantise = to_quantise[1:]
